import numpy as np
import ml_dtypes


def mxq(x, axis, fmt="e4m3"):
    dtype, down = {"e4m3": (ml_dtypes.float8_e4m3fn, 7), "e5m2": (ml_dtypes.float8_e5m2, 14)}[fmt]
    v = np.moveaxis(np.asarray(x, np.float32).astype(ml_dtypes.bfloat16).astype(np.float64), axis, -1)
    blocks = v.reshape(v.shape[:-1] + (-1, 32))
    amax = np.abs(blocks).max(-1, keepdims=True)
    byte = np.maximum(np.where(amax > 0, np.frexp(amax)[1] - 1 + 127, 0) - down, 1)
    scale = np.exp2(byte - 127.0)
    codes = (blocks / scale).astype(np.float32).astype(dtype).astype(np.float64)
    return np.moveaxis((codes * scale).reshape(v.shape), -1, axis)


WIDE = False


def mx_kscale(k):
    if not WIDE:
        return np.ones(k)
    levels = np.array([10, -10, 5, -5, 0])
    a = np.random.permutation(np.resize(levels, k // 512 * 4)).reshape(k // 512, 4)
    idx = np.arange(k)
    return np.exp2(a[idx // 512, idx % 128 // 32])


BF16 = ml_dtypes.bfloat16


def bf(x):
    return np.asarray(x, np.float32).astype(BF16)


def f64(x):
    return np.asarray(x).astype(np.float64)


B, H, W, C = 128, 5, 5, 1024
G = C // 4
NBR = 3


def setup_inputs():
    s = mx_kscale(C)
    return {
        "h_mix": bf(0.8 * np.random.standard_normal((B, H, W, C)) * s),
        "w_mix": bf(0.8 * np.random.standard_normal((B, H, W, C)) * s),
        "c_proj": bf(np.random.standard_normal((B, H, W, C)) * s),
        "gate_hid": bf(0.6 * np.random.standard_normal((B, G))),
        "wa2": bf(2.0 * np.random.standard_normal((G, C * NBR)) / np.sqrt(G)),
        "ba2": bf(0.6 * np.random.standard_normal(C * NBR)),
        "wo": bf(np.random.standard_normal((C, C)) / np.sqrt(C) / s[:, None]),
        "bo": bf(0.3 * np.random.standard_normal(C)),
    }


def reference(h_mix, w_mix, c_proj, gate_hid, wa2, ba2, wo, bo):
    z = f64(gate_hid) @ f64(wa2) + f64(ba2)
    z = z.reshape(B, C, NBR).transpose(2, 0, 1)
    e = np.exp(z - z.max(0, keepdims=True))
    a = (e / e.sum(0, keepdims=True))[:, :, None, None, :]
    fused = f64(h_mix) * a[0] + f64(w_mix) * a[1] + f64(c_proj) * a[2]
    return (mxq(fused, 3, "e4m3") @ mxq(f64(wo), 0, "e4m3")) + f64(bo)

@@ -1,0 +1,182 @@
+from contextlib import ExitStack
+
+import concourse.mybir as mybir
+from concourse.masks import make_identity
+
+F32 = mybir.dt.float32
+BF16 = mybir.dt.bfloat16
+U32 = mybir.dt.uint32
+U8 = mybir.dt.uint8
+FP8X4 = mybir.dt.float8_e4m3fn_x4
+ALU = mybir.AluOpType
+ACT = mybir.ActivationFunctionType
+
+P = 128
+B, HW, C, GH, NBR = 128, 25, 1024, 256, 3
+HALF = 512
+CH = 5
+NCH = HW // CH
+XBUFS = 3
+GROUPS = ((0, 1), (1, 2), (3, 2))
+
+FLOPS = 2 * B * HW * C * C + 2 * B * GH * NBR * C
+
+
+def tile_hiremodule_pc_kernel(tc, h_mix, w_mix, c_proj, gate_hid, wa2, ba2, wo, bo, out):
+    nc = tc.nc
+    xv = [x.rearrange("b i j c -> b (i j) c") for x in (h_mix, w_mix, c_proj)]
+    outv = out.rearrange("b i j c -> b (i j) c")
+
+    with ExitStack() as ctx:
+        consts = ctx.enter_context(tc.tile_pool(name="consts", bufs=1))
+        xpool = ctx.enter_context(tc.tile_pool(name="xpool", bufs=XBUFS))
+        ppool = ctx.enter_context(tc.tile_pool(name="ppool", bufs=3))
+        psum = ctx.enter_context(tc.psum_pool(name="psum", bufs=1))
+
+        ident_f = consts.tile([P, P], F32, name="ident_f")
+        ident_b = consts.tile([P, P], BF16, name="ident_b")
+        a_sb = consts.tile([P, NBR, C], F32, name="a_sb")
+        bo_bc = consts.tile([P, C], BF16, name="bo_bc")
+        w_codes = consts.tile([P, 2, C], U32, name="w_codes", align_bytes=64)
+        w_scales = consts.tile([P, 2, C], U8, name="w_scales", align_bytes=64)
+
+        xt = {}
+
+        def load_chunk(c):
+            for k in range(NBR):
+                t = xpool.tile([P, CH, C], BF16, tag="x%d" % k, name="x%d_%d" % (k, c))
+                nc.sync.dma_start(out=t[:], in_=xv[k][:, c * CH:(c + 1) * CH, :])
+                xt[(k, c)] = t
+
+        z_tags = (("pa", "pd"), ("pb", "pe"), ("pc", "pf"))
+        a_ps = [[None, None], [None, None]]
+
+        with tc.tile_pool(name="head", bufs=1) as head:
+            make_identity(nc, ident_b[:])
+            make_identity(nc, ident_f[:])
+
+            gh = head.tile([P, GH], BF16, name="gh")
+            nc.sync.dma_start(out=gh[:], in_=gate_hid)
+            ba_rows = head.tile([P, NBR * C], BF16, name="ba_rows")
+            nc.vector.memset(ba_rows[:], 0.0)
+            nc.sync.dma_start(out=ba_rows[0:1, :], in_=ba2.rearrange("(o c) -> o c", o=1))
+            wa = head.tile([P, 2, NBR * C], BF16, name="wa")
+            wav = wa2.rearrange("(kc p) c -> p kc c", p=P)
+            for hf in range(2):
+                cols = slice(hf * NBR * HALF, (hf + 1) * NBR * HALF)
+                nc.sync.dma_start(out=wa[:, :, cols], in_=wav[:, :, cols])
+            wo_raw = head.tile([P, 2, 4, C], BF16, name="wo_raw")
+            nc.sync.dma_start(out=wo_raw[:], in_=wo.rearrange("(g t p) n -> p g t n", g=2, t=4, p=P))
+            nc.sync.dma_start(out=bo_bc[:], in_=bo.partition_broadcast(P))
+            for c in range(XBUFS):
+                load_chunk(c)
+
+            ones_b = head.tile([P, P], BF16, name="ones_b")
+            nc.vector.memset(ones_b[:], 1.0)
+            warm = head.tile([P, 1], F32, name="warm")
+            nc.vector.memset(warm[:], 0.0)
+            nc.scalar.activation(out=warm[:], in_=warm[:], func=ACT.Exp)
+
+            ght_ps = psum.tile([P, 2, P], BF16, tag="pg", name="ght_ps")
+            for kc in range(2):
+                nc.tensor.transpose(ght_ps[:, kc, :], gh[:, kc * P:(kc + 1) * P], ident_b[:])
+            ght = head.tile([P, 2, P], BF16, name="ght")
+            nc.vector.tensor_copy(out=ght[:], in_=ght_ps[:])
+
+            for hf in range(2):
+                cols = slice(hf * NBR * HALF, (hf + 1) * NBR * HALF)
+                z = []
+                for k in range(NBR):
+                    zt = psum.tile([P, HALF], F32, tag=z_tags[k][hf], name="z%d_%d" % (k, hf))
+                    nc.tensor.matmul(
+                        zt[:], lhsT=ones_b[:],
+                        rhs=ba_rows[:, cols].rearrange("p (c k) -> p c k", k=NBR)[:, :, k],
+                        start=True, stop=False)
+                    for kc in range(2):
+                        nc.tensor.matmul(
+                            zt[:], lhsT=ght[:, kc, :],
+                            rhs=wa[:, kc, cols].rearrange("p (c k) -> p c k", k=NBR)[:, :, k],
+                            start=False, stop=(kc == 1))
+                    z.append(zt)
+                zs0 = head.tile([P, HALF], F32, name="zs0_%d" % hf)
+                nc.scalar.copy(out=zs0[:], in_=z[0][:])
+                m = head.tile([P, HALF], F32, name="m_%d" % hf)
+                nc.vector.tensor_tensor(out=m[:], in0=z[1][:], in1=zs0[:], op=ALU.max)
+                nc.vector.tensor_tensor(out=m[:], in0=z[2][:], in1=m[:], op=ALU.max)
+                e = head.tile([P, NBR, HALF], F32, name="e_%d" % hf)
+                for k in range(NBR):
+                    nc.vector.tensor_tensor(out=e[:, k, :], in0=z[k][:], in1=m[:], op=ALU.subtract)
+                nc.scalar.activation(out=e[:], in_=e[:], func=ACT.Exp)
+                s = head.tile([P, HALF], F32, name="s_%d" % hf)
+                nc.vector.tensor_tensor(out=s[:], in0=e[:, 0, :], in1=e[:, 1, :], op=ALU.add)
+                nc.vector.tensor_tensor(out=s[:], in0=s[:], in1=e[:, 2, :], op=ALU.add)
+                nc.vector.reciprocal(out=s[:], in_=s[:])
+                nc.vector.tensor_tensor(
+                    out=a_sb[:, :, hf * HALF:(hf + 1) * HALF], in0=e[:],
+                    in1=s[:].unsqueeze(1).to_broadcast([P, NBR, HALF]), op=ALU.mult)
+                for k in range(2):
+                    ap = psum.tile([P, HALF], F32, tag=z_tags[k][hf], name="aps%d_%d" % (k, hf))
+                    nc.tensor.matmul(ap[:], lhsT=ident_f[:], rhs=a_sb[:, k, hf * HALF:(hf + 1) * HALF],
+                                     start=True, stop=True)
+                    a_ps[k][hf] = ap
+
+            for g in range(2):
+                wo_grp = head.tile([P, C, 4], BF16, tag="wo_grp", name="wo_grp%d" % g, align_bytes=64)
+                for nh in range(2):
+                    ns = slice(nh * HALF, (nh + 1) * HALF)
+                    nc.scalar.copy(out=wo_grp[:, ns, :], in_=wo_raw[:, g, :, ns].rearrange("p t n -> p n t"))
+                nc.vector.quantize_mx(
+                    out=w_codes[:, g, :].bitcast(FP8X4), scales=w_scales[:, g, :],
+                    in_=wo_grp[:].rearrange("p n t -> p (n t)"))
+
+        gpool = ctx.enter_context(tc.tile_pool(name="gpool", bufs=3))
+        opool = ctx.enter_context(tc.tile_pool(name="opool", bufs=4))
+        acc_tags = ("pg", "ph")
+        o_tags = ("pc", "pf")
+
+        for c in range(NCH):
+            for (j0, n) in GROUPS:
+                p2 = ppool.tile([P, n, C], F32, tag="p2", name="p2_%d_%d" % (c, j0))
+                nc.gpsimd.tensor_tensor(
+                    out=p2[:], in0=xt[(2, c)][:, j0:j0 + n, :],
+                    in1=a_sb[:, 2, :].unsqueeze(1).to_broadcast([P, n, C]), op=ALU.mult)
+                for jj in range(n):
+                    j = j0 + jj
+                    ij = c * CH + j
+                    pv = []
+                    for k in range(2):
+                        pk = ppool.tile([P, C], F32, tag="p%d" % k, name="p%d_%d" % (k, ij))
+                        for hf in range(2):
+                            hs = slice(hf * HALF, (hf + 1) * HALF)
+                            nc.vector.tensor_tensor(out=pk[:, hs], in0=xt[(k, c)][:, j, hs],
+                                                    in1=a_ps[k][hf][:], op=ALU.mult)
+                        pv.append(pk[:])
+                    pv.append(p2[:, jj, :])
+
+                    grp = gpool.tile([P, 2, P, 4], BF16, tag="grp", name="grp%d" % ij, align_bytes=64)
+                    for g in range(2):
+                        acc = psum.tile([P, 4, P], F32, tag=acc_tags[g], name="acc%d_%d" % (g, ij))
+                        for t in range(4):
+                            col = (4 * g + t) * P
+                            for k in range(NBR):
+                                nc.tensor.matmul(acc[:, t, :], lhsT=pv[k][:, col:col + P], rhs=ident_f[:],
+                                                 is_transpose=True, start=(k == 0), stop=(k == NBR - 1))
+                        nc.scalar.copy(out=grp[:, g, :, :], in_=acc[:].rearrange("p t b -> p b t"))
+                    codes = gpool.tile([P, 2 * P], U32, tag="codes", name="codes%d" % ij, align_bytes=64)
+                    scl = gpool.tile([P, 2 * P], U8, tag="scl", name="scl%d" % ij, align_bytes=64)
+                    nc.vector.quantize_mx(out=codes[:].bitcast(FP8X4), scales=scl[:],
+                                          in_=grp[:].rearrange("p g b t -> p (g b t)"))
+                    ost = opool.tile([P, C], F32, tag="ost", name="ost%d" % ij)
+                    for nh in range(2):
+                        ns = slice(nh * HALF, (nh + 1) * HALF)
+                        o = psum.tile([P, HALF], F32, tag=o_tags[nh], name="o%d_%d" % (nh, ij))
+                        for g in range(2):
+                            gs = slice(g * P, (g + 1) * P)
+                            nc.tensor.matmul_mx(
+                                out=o[:], lhsT=codes[:, gs].bitcast(FP8X4), lhsT_scale=scl[:, gs],
+                                rhs=w_codes[:, g, ns].bitcast(FP8X4), rhs_scale=w_scales[:, g, ns],
+                                start=(g == 0), stop=(g == 1))
+                        nc.vector.tensor_tensor(out=ost[:, ns], in0=o[:], in1=bo_bc[:, ns], op=ALU.add)
+                    nc.sync.dma_start(out=outv[:, ij, :], in_=ost[:])
+            if c + XBUFS < NCH:
+                load_chunk(c + XBUFS)

@@ -14,10 +14,10 @@ ACT = mybir.ActivationFunctionType
 P = 128
 B, HW, C, GH, NBR = 128, 25, 1024, 256, 3
 HALF = 512
-CH = 5
-NCH = HW // CH
 XBUFS = 3
-GROUPS = ((0, 1), (1, 2), (3, 2))
+CHUNKS = ((0, 5), (5, 4), (9, 4), (13, 4), (17, 4), (21, 4))
+BLOCKS = ((0, 1),) + tuple((1 + 2 * i, 2) for i in range(11)) + ((23, 1), (24, 1))
+NB = len(BLOCKS)
 
 FLOPS = 2 * B * HW * C * C + 2 * B * GH * NBR * C
 
@@ -30,7 +30,7 @@ def tile_hiremodule_pc_kernel(tc, h_mix, w_mix, c_proj, gate_hid, wa2, ba2, wo, 
     with ExitStack() as ctx:
         consts = ctx.enter_context(tc.tile_pool(name="consts", bufs=1))
         xpool = ctx.enter_context(tc.tile_pool(name="xpool", bufs=XBUFS))
-        ppool = ctx.enter_context(tc.tile_pool(name="ppool", bufs=3))
+        ppool = ctx.enter_context(tc.tile_pool(name="ppool", bufs=2))
         psum = ctx.enter_context(tc.psum_pool(name="psum", bufs=1))
 
         ident_f = consts.tile([P, P], F32, name="ident_f")
@@ -43,13 +43,14 @@ def tile_hiremodule_pc_kernel(tc, h_mix, w_mix, c_proj, gate_hid, wa2, ba2, wo, 
         xt = {}
 
         def load_chunk(c):
+            i0, cn = CHUNKS[c]
             for k in range(NBR):
-                t = xpool.tile([P, CH, C], BF16, tag="x%d" % k, name="x%d_%d" % (k, c))
-                nc.sync.dma_start(out=t[:], in_=xv[k][:, c * CH:(c + 1) * CH, :])
+                t = xpool.tile([P, cn, C], BF16, tag="x%d" % k, name="x%d_%d" % (k, c))
+                nc.sync.dma_start(out=t[:], in_=xv[k][:, i0:i0 + cn, :])
                 xt[(k, c)] = t
 
-        z_tags = (("pa", "pd"), ("pb", "pe"), ("pc", "pf"))
-        a_ps = [[None, None], [None, None]]
+        z_tags = (("pa", "pb"), ("pc", "o"), ("o", "o"))
+        a_ps = {}
 
         with tc.tile_pool(name="head", bufs=1) as head:
             make_identity(nc, ident_b[:])
@@ -77,7 +78,7 @@ def tile_hiremodule_pc_kernel(tc, h_mix, w_mix, c_proj, gate_hid, wa2, ba2, wo, 
             nc.vector.memset(warm[:], 0.0)
             nc.scalar.activation(out=warm[:], in_=warm[:], func=ACT.Exp)
 
-            ght_ps = psum.tile([P, 2, P], BF16, tag="pg", name="ght_ps")
+            ght_ps = psum.tile([P, 2, P], BF16, tag="acc0", name="ght_ps")
             for kc in range(2):
                 nc.tensor.transpose(ght_ps[:, kc, :], gh[:, kc * P:(kc + 1) * P], ident_b[:])
             ght = head.tile([P, 2, P], BF16, name="ght")
@@ -87,7 +88,8 @@ def tile_hiremodule_pc_kernel(tc, h_mix, w_mix, c_proj, gate_hid, wa2, ba2, wo, 
                 cols = slice(hf * NBR * HALF, (hf + 1) * NBR * HALF)
                 z = []
                 for k in range(NBR):
-                    zt = psum.tile([P, HALF], F32, tag=z_tags[k][hf], name="z%d_%d" % (k, hf))
+                    zt = psum.tile([P, HALF], F32, tag=z_tags[k][hf], name="z%d_%d" % (k, hf),
+                                   bufs=(3 if z_tags[k][hf] == "o" else 1))
                     nc.tensor.matmul(
                         zt[:], lhsT=ones_b[:],
                         rhs=ba_rows[:, cols].rearrange("p (c k) -> p c k", k=NBR)[:, :, k],
@@ -114,11 +116,11 @@ def tile_hiremodule_pc_kernel(tc, h_mix, w_mix, c_proj, gate_hid, wa2, ba2, wo, 
                 nc.vector.tensor_tensor(
                     out=a_sb[:, :, hf * HALF:(hf + 1) * HALF], in0=e[:],
                     in1=s[:].unsqueeze(1).to_broadcast([P, NBR, HALF]), op=ALU.mult)
-                for k in range(2):
+                for k in range(2 - hf):
                     ap = psum.tile([P, HALF], F32, tag=z_tags[k][hf], name="aps%d_%d" % (k, hf))
                     nc.tensor.matmul(ap[:], lhsT=ident_f[:], rhs=a_sb[:, k, hf * HALF:(hf + 1) * HALF],
                                      start=True, stop=True)
-                    a_ps[k][hf] = ap
+                    a_ps[(k, hf)] = ap
 
             for g in range(2):
                 wo_grp = head.tile([P, C, 4], BF16, tag="wo_grp", name="wo_grp%d" % g, align_bytes=64)
@@ -130,53 +132,112 @@ def tile_hiremodule_pc_kernel(tc, h_mix, w_mix, c_proj, gate_hid, wa2, ba2, wo, 
                     in_=wo_grp[:].rearrange("p n t -> p (n t)"))
 
         gpool = ctx.enter_context(tc.tile_pool(name="gpool", bufs=3))
-        opool = ctx.enter_context(tc.tile_pool(name="opool", bufs=4))
-        acc_tags = ("pg", "ph")
-        o_tags = ("pc", "pf")
+        opool = ctx.enter_context(tc.tile_pool(name="opool", bufs=3))
 
-        for c in range(NCH):
-            for (j0, n) in GROUPS:
-                p2 = ppool.tile([P, n, C], F32, tag="p2", name="p2_%d_%d" % (c, j0))
-                nc.gpsimd.tensor_tensor(
-                    out=p2[:], in0=xt[(2, c)][:, j0:j0 + n, :],
-                    in1=a_sb[:, 2, :].unsqueeze(1).to_broadcast([P, n, C]), op=ALU.mult)
-                for jj in range(n):
-                    j = j0 + jj
-                    ij = c * CH + j
-                    pv = []
-                    for k in range(2):
-                        pk = ppool.tile([P, C], F32, tag="p%d" % k, name="p%d_%d" % (k, ij))
-                        for hf in range(2):
-                            hs = slice(hf * HALF, (hf + 1) * HALF)
-                            nc.vector.tensor_tensor(out=pk[:, hs], in0=xt[(k, c)][:, j, hs],
-                                                    in1=a_ps[k][hf][:], op=ALU.mult)
-                        pv.append(pk[:])
-                    pv.append(p2[:, jj, :])
+        def where(ij):
+            for c in range(len(CHUNKS)):
+                i0, cn = CHUNKS[c]
+                if i0 <= ij < i0 + cn:
+                    return c, ij - i0
+            return None
 
-                    grp = gpool.tile([P, 2, P, 4], BF16, tag="grp", name="grp%d" % ij, align_bytes=64)
-                    for g in range(2):
-                        acc = psum.tile([P, 4, P], F32, tag=acc_tags[g], name="acc%d_%d" % (g, ij))
-                        for t in range(4):
-                            col = (4 * g + t) * P
-                            for k in range(NBR):
-                                nc.tensor.matmul(acc[:, t, :], lhsT=pv[k][:, col:col + P], rhs=ident_f[:],
-                                                 is_transpose=True, start=(k == 0), stop=(k == NBR - 1))
-                        nc.scalar.copy(out=grp[:, g, :, :], in_=acc[:].rearrange("p t b -> p b t"))
-                    codes = gpool.tile([P, 2 * P], U32, tag="codes", name="codes%d" % ij, align_bytes=64)
-                    scl = gpool.tile([P, 2 * P], U8, tag="scl", name="scl%d" % ij, align_bytes=64)
-                    nc.vector.quantize_mx(out=codes[:].bitcast(FP8X4), scales=scl[:],
-                                          in_=grp[:].rearrange("p g b t -> p (g b t)"))
-                    ost = opool.tile([P, C], F32, tag="ost", name="ost%d" % ij)
-                    for nh in range(2):
-                        ns = slice(nh * HALF, (nh + 1) * HALF)
-                        o = psum.tile([P, HALF], F32, tag=o_tags[nh], name="o%d_%d" % (nh, ij))
-                        for g in range(2):
-                            gs = slice(g * P, (g + 1) * P)
-                            nc.tensor.matmul_mx(
-                                out=o[:], lhsT=codes[:, gs].bitcast(FP8X4), lhsT_scale=scl[:, gs],
-                                rhs=w_codes[:, g, ns].bitcast(FP8X4), rhs_scale=w_scales[:, g, ns],
-                                start=(g == 0), stop=(g == 1))
-                        nc.vector.tensor_tensor(out=ost[:, ns], in0=o[:], in1=bo_bc[:, ns], op=ALU.add)
-                    nc.sync.dma_start(out=outv[:, ij, :], in_=ost[:])
-            if c + XBUFS < NCH:
-                load_chunk(c + XBUFS)
+        prod = {}
+        quant = {}
+        stage = {}
+
+        def m_gpsimd(q):
+            ij0, n = BLOCKS[q]
+            c, j0 = where(ij0)
+            for k in range(NBR):
+                prod[(q, k)] = ppool.tile([P, n, C], F32, tag="p%d" % k, name="p%d_%d" % (k, q))
+            nc.gpsimd.tensor_tensor(
+                out=prod[(q, 1)][:, :, HALF:C], in0=xt[(1, c)][:, j0:j0 + n, HALF:C],
+                in1=a_sb[:, 1, HALF:C].unsqueeze(1).to_broadcast([P, n, HALF]), op=ALU.mult)
+            nc.gpsimd.tensor_tensor(
+                out=prod[(q, 2)][:], in0=xt[(2, c)][:, j0:j0 + n, :],
+                in1=a_sb[:, 2, :].unsqueeze(1).to_broadcast([P, n, C]), op=ALU.mult)
+
+        def m_vector(q, k, hf):
+            ij0, n = BLOCKS[q]
+            c, j0 = where(ij0)
+            hs = slice(hf * HALF, (hf + 1) * HALF)
+            nc.vector.tensor_tensor(
+                out=prod[(q, k)][:, :, hs], in0=xt[(k, c)][:, j0:j0 + n, hs],
+                in1=a_ps[(k, hf)][:].unsqueeze(1).to_broadcast([P, n, HALF]), op=ALU.mult)
+
+        V_PIECES = ((0, 1), (0, 0), (1, 0))
+
+        def t_run(q, jj, g):
+            n = BLOCKS[q][1]
+            if (jj, g) == (0, 0):
+                quant[q] = (
+                    gpool.tile([P, n, 2, P, 4], BF16, tag="grp", name="grp%d" % q, align_bytes=64),
+                    gpool.tile([P, n * 2 * P], U32, tag="codes", name="codes%d" % q, align_bytes=64),
+                    gpool.tile([P, n * 2 * P], U8, tag="scl", name="scl%d" % q, align_bytes=64),
+                )
+            acc = psum.tile([P, 4, P], F32, tag="acc%d" % g, name="acc%d_%d_%d" % (g, q, jj))
+            for t in range(4):
+                col = (4 * g + t) * P
+                for k in (2, 1, 0):
+                    nc.tensor.matmul(acc[:, t, :], lhsT=prod[(q, k)][:, jj, col:col + P], rhs=ident_f[:],
+                                     is_transpose=True, start=(k == 2), stop=(k == 0))
+            nc.scalar.copy(out=quant[q][0][:, jj, g, :, :], in_=acc[:].rearrange("p t b -> p b t"))
+
+        def quantise(q):
+            grp, codes, scl = quant[q]
+            nc.vector.quantize_mx(out=codes[:].bitcast(FP8X4), scales=scl[:],
+                                  in_=grp[:].rearrange("p j g b t -> p (j g b t)"))
+
+        def mx_pair(q, jj, nh):
+            codes, scl = quant[q][1], quant[q][2]
+            ns = slice(nh * HALF, (nh + 1) * HALF)
+            o = psum.tile([P, HALF], F32, tag="o", name="o%d_%d_%d" % (nh, q, jj), bufs=3)
+            for g in range(2):
+                gs = slice((2 * jj + g) * P, (2 * jj + g + 1) * P)
+                nc.tensor.matmul_mx(
+                    out=o[:], lhsT=codes[:, gs].bitcast(FP8X4), lhsT_scale=scl[:, gs],
+                    rhs=w_codes[:, g, ns].bitcast(FP8X4), rhs_scale=w_scales[:, g, ns],
+                    start=(g == 0), stop=(g == 1))
+            return o
+
+        def add_bias(q, jj, nh, o):
+            ij0, n = BLOCKS[q]
+            if (jj, nh) == (0, 0):
+                stage[q] = opool.tile([P, n, C], F32, tag="ost", name="ost%d" % q)
+            ns = slice(nh * HALF, (nh + 1) * HALF)
+            nc.vector.tensor_tensor(out=stage[q][:, jj, ns], in0=o[:], in1=bo_bc[:, ns], op=ALU.add)
+            if (jj, nh) == (n - 1, 1):
+                nc.sync.dma_start(out=outv[:, ij0:ij0 + n, :], in_=stage[q][:])
+
+        with tc.manual_schedule():
+            m_gpsimd(0)
+            for (k, hf) in V_PIECES:
+                m_vector(0, k, hf)
+            late = []
+            for q in range(NB + 1):
+                if q + 1 < NB:
+                    m_gpsimd(q + 1)
+                if q >= 1:
+                    quantise(q - 1)
+                for item in late:
+                    add_bias(item[0], item[1], item[2], item[3])
+                late = []
+                runs = [(jj, g) for jj in range(BLOCKS[q][1]) for g in range(2)] if q < NB else []
+                pairs = [(jj, nh) for jj in range(BLOCKS[q - 1][1]) for nh in range(2)] if q >= 1 else []
+                pieces = list(V_PIECES) if q + 1 < NB else []
+                for r in range(max(len(runs), len(pairs), len(pieces))):
+                    if r < len(runs):
+                        t_run(q, runs[r][0], runs[r][1])
+                    if r < len(pieces):
+                        m_vector(q + 1, pieces[r][0], pieces[r][1])
+                    if r < len(pairs):
+                        o = mx_pair(q - 1, pairs[r][0], pairs[r][1])
+                        if r == len(pairs) - 1 and q < NB:
+                            late.append((q - 1, pairs[r][0], pairs[r][1], o))
+                        else:
+                            add_bias(q - 1, pairs[r][0], pairs[r][1], o)
+                if q + 1 < NB:
+                    ij_end = BLOCKS[q + 1][0] + BLOCKS[q + 1][1]
+                    for c in range(len(CHUNKS) - XBUFS):
+                        if CHUNKS[c][0] + CHUNKS[c][1] == ij_end:
+                            load_chunk(c + XBUFS)

@@ -213,29 +213,22 @@ def tile_hiremodule_pc_kernel(tc, h_mix, w_mix, c_proj, gate_hid, wa2, ba2, wo, 
             m_gpsimd(0)
             for (k, hf) in V_PIECES:
                 m_vector(0, k, hf)
-            late = []
             for q in range(NB + 1):
                 if q + 1 < NB:
                     m_gpsimd(q + 1)
                 if q >= 1:
                     quantise(q - 1)
-                for item in late:
-                    add_bias(item[0], item[1], item[2], item[3])
-                late = []
-                runs = [(jj, g) for jj in range(BLOCKS[q][1]) for g in range(2)] if q < NB else []
-                pairs = [(jj, nh) for jj in range(BLOCKS[q - 1][1]) for nh in range(2)] if q >= 1 else []
-                pieces = list(V_PIECES) if q + 1 < NB else []
-                for r in range(max(len(runs), len(pairs), len(pieces))):
-                    if r < len(runs):
-                        t_run(q, runs[r][0], runs[r][1])
-                    if r < len(pieces):
-                        m_vector(q + 1, pieces[r][0], pieces[r][1])
-                    if r < len(pairs):
-                        o = mx_pair(q - 1, pairs[r][0], pairs[r][1])
-                        if r == len(pairs) - 1 and q < NB:
-                            late.append((q - 1, pairs[r][0], pairs[r][1], o))
-                        else:
-                            add_bias(q - 1, pairs[r][0], pairs[r][1], o)
+                if q + 1 < NB:
+                    for (k, hf) in V_PIECES:
+                        m_vector(q + 1, k, hf)
+                if q < NB:
+                    for jj in range(BLOCKS[q][1]):
+                        for g in range(2):
+                            t_run(q, jj, g)
+                if q >= 1:
+                    for jj in range(BLOCKS[q - 1][1]):
+                        for nh in range(2):
+                            add_bias(q - 1, jj, nh, mx_pair(q - 1, jj, nh))
                 if q + 1 < NB:
                     ij_end = BLOCKS[q + 1][0] + BLOCKS[q + 1][1]
                     for c in range(len(CHUNKS) - XBUFS):

@@ -167,21 +167,23 @@ def tile_hiremodule_pc_kernel(tc, h_mix, w_mix, c_proj, gate_hid, wa2, ba2, wo, 
 
         V_PIECES = ((0, 1), (0, 0), (1, 0))
 
-        def t_run(q, jj, g):
+        def t_run(q, jj):
             n = BLOCKS[q][1]
-            if (jj, g) == (0, 0):
+            if jj == 0:
                 quant[q] = (
                     gpool.tile([P, n, 2, P, 4], BF16, tag="grp", name="grp%d" % q, align_bytes=64),
                     gpool.tile([P, n * 2 * P], U32, tag="codes", name="codes%d" % q, align_bytes=64),
                     gpool.tile([P, n * 2 * P], U8, tag="scl", name="scl%d" % q, align_bytes=64),
                 )
-            acc = psum.tile([P, 4, P], F32, tag="acc%d" % g, name="acc%d_%d_%d" % (g, q, jj))
-            for t in range(4):
-                col = (4 * g + t) * P
-                for k in (2, 1, 0):
-                    nc.tensor.matmul(acc[:, t, :], lhsT=prod[(q, k)][:, jj, col:col + P], rhs=ident_f[:],
-                                     is_transpose=True, start=(k == 2), stop=(k == 0))
-            nc.scalar.copy(out=quant[q][0][:, jj, g, :, :], in_=acc[:].rearrange("p t b -> p b t"))
+            acc = [psum.tile([P, 4, P], F32, tag="acc%d" % g, name="acc%d_%d_%d" % (g, q, jj)) for g in range(2)]
+            for k in (2, 1, 0):
+                for t in range(4):
+                    for g in range(2):
+                        col = (4 * g + t) * P
+                        nc.tensor.matmul(acc[g][:, t, :], lhsT=prod[(q, k)][:, jj, col:col + P], rhs=ident_f[:],
+                                         is_transpose=True, start=(k == 2 and t == 0), stop=(k == 0 and t == 3))
+            for g in range(2):
+                nc.scalar.copy(out=quant[q][0][:, jj, g, :, :], in_=acc[g][:].rearrange("p t b -> p b t"))
 
         def quantise(q):
             grp, codes, scl = quant[q]
@@ -218,17 +220,21 @@ def tile_hiremodule_pc_kernel(tc, h_mix, w_mix, c_proj, gate_hid, wa2, ba2, wo, 
                     m_gpsimd(q + 1)
                 if q >= 1:
                     quantise(q - 1)
-                if q + 1 < NB:
-                    for (k, hf) in V_PIECES:
+                pieces = list(V_PIECES) if q + 1 < NB else []
+                n_t = BLOCKS[q][1] if q < NB else 0
+                n_x = BLOCKS[q - 1][1] if q >= 1 else 0
+                for jj in range(max(n_t, n_x)):
+                    if jj < n_t:
+                        t_run(q, jj)
+                    take = 2 if jj == 0 else 1
+                    for (k, hf) in pieces[:take]:
                         m_vector(q + 1, k, hf)
-                if q < NB:
-                    for jj in range(BLOCKS[q][1]):
-                        for g in range(2):
-                            t_run(q, jj, g)
-                if q >= 1:
-                    for jj in range(BLOCKS[q - 1][1]):
+                    pieces = pieces[take:]
+                    if jj < n_x:
                         for nh in range(2):
                             add_bias(q - 1, jj, nh, mx_pair(q - 1, jj, nh))
+                for (k, hf) in pieces:
+                    m_vector(q + 1, k, hf)
                 if q + 1 < NB:
                     ij_end = BLOCKS[q + 1][0] + BLOCKS[q + 1][1]
                     for c in range(len(CHUNKS) - XBUFS):

@@ -49,7 +49,7 @@ def tile_hiremodule_pc_kernel(tc, h_mix, w_mix, c_proj, gate_hid, wa2, ba2, wo, 
                 nc.sync.dma_start(out=t[:], in_=xv[k][:, i0:i0 + cn, :])
                 xt[(k, c)] = t
 
-        z_tags = (("pa", "pb"), ("pc", "o"), ("o", "o"))
+        z_tags = (("pa", "pb"), ("pc", "pd"), ("o", "o"))
         a_ps = {}
 
         with tc.tile_pool(name="head", bufs=1) as head:
@@ -89,7 +89,7 @@ def tile_hiremodule_pc_kernel(tc, h_mix, w_mix, c_proj, gate_hid, wa2, ba2, wo, 
                 z = []
                 for k in range(NBR):
                     zt = psum.tile([P, HALF], F32, tag=z_tags[k][hf], name="z%d_%d" % (k, hf),
-                                   bufs=(3 if z_tags[k][hf] == "o" else 1))
+                                   bufs=(2 if z_tags[k][hf] == "o" else 1))
                     nc.tensor.matmul(
                         zt[:], lhsT=ones_b[:],
                         rhs=ba_rows[:, cols].rearrange("p (c k) -> p c k", k=NBR)[:, :, k],
@@ -116,7 +116,7 @@ def tile_hiremodule_pc_kernel(tc, h_mix, w_mix, c_proj, gate_hid, wa2, ba2, wo, 
                 nc.vector.tensor_tensor(
                     out=a_sb[:, :, hf * HALF:(hf + 1) * HALF], in0=e[:],
                     in1=s[:].unsqueeze(1).to_broadcast([P, NBR, HALF]), op=ALU.mult)
-                for k in range(2 - hf):
+                for k in range(2):
                     ap = psum.tile([P, HALF], F32, tag=z_tags[k][hf], name="aps%d_%d" % (k, hf))
                     nc.tensor.matmul(ap[:], lhsT=ident_f[:], rhs=a_sb[:, k, hf * HALF:(hf + 1) * HALF],
                                      start=True, stop=True)
@@ -151,9 +151,6 @@ def tile_hiremodule_pc_kernel(tc, h_mix, w_mix, c_proj, gate_hid, wa2, ba2, wo, 
             for k in range(NBR):
                 prod[(q, k)] = ppool.tile([P, n, C], F32, tag="p%d" % k, name="p%d_%d" % (k, q))
             nc.gpsimd.tensor_tensor(
-                out=prod[(q, 1)][:, :, HALF:C], in0=xt[(1, c)][:, j0:j0 + n, HALF:C],
-                in1=a_sb[:, 1, HALF:C].unsqueeze(1).to_broadcast([P, n, HALF]), op=ALU.mult)
-            nc.gpsimd.tensor_tensor(
                 out=prod[(q, 2)][:], in0=xt[(2, c)][:, j0:j0 + n, :],
                 in1=a_sb[:, 2, :].unsqueeze(1).to_broadcast([P, n, C]), op=ALU.mult)
 
@@ -165,25 +162,23 @@ def tile_hiremodule_pc_kernel(tc, h_mix, w_mix, c_proj, gate_hid, wa2, ba2, wo, 
                 out=prod[(q, k)][:, :, hs], in0=xt[(k, c)][:, j0:j0 + n, hs],
                 in1=a_ps[(k, hf)][:].unsqueeze(1).to_broadcast([P, n, HALF]), op=ALU.mult)
 
-        V_PIECES = ((0, 1), (0, 0), (1, 0))
+        V_PIECES = ((0, 1), (0, 0), (1, 1), (1, 0))
 
-        def t_run(q, jj):
+        def t_run(q, jj, g):
             n = BLOCKS[q][1]
-            if jj == 0:
+            if (jj, g) == (0, 0):
                 quant[q] = (
                     gpool.tile([P, n, 2, P, 4], BF16, tag="grp", name="grp%d" % q, align_bytes=64),
                     gpool.tile([P, n * 2 * P], U32, tag="codes", name="codes%d" % q, align_bytes=64),
                     gpool.tile([P, n * 2 * P], U8, tag="scl", name="scl%d" % q, align_bytes=64),
                 )
-            acc = [psum.tile([P, 4, P], F32, tag="acc%d" % g, name="acc%d_%d_%d" % (g, q, jj)) for g in range(2)]
-            for k in (2, 1, 0):
-                for t in range(4):
-                    for g in range(2):
-                        col = (4 * g + t) * P
-                        nc.tensor.matmul(acc[g][:, t, :], lhsT=prod[(q, k)][:, jj, col:col + P], rhs=ident_f[:],
-                                         is_transpose=True, start=(k == 2 and t == 0), stop=(k == 0 and t == 3))
-            for g in range(2):
-                nc.scalar.copy(out=quant[q][0][:, jj, g, :, :], in_=acc[g][:].rearrange("p t b -> p b t"))
+            acc = psum.tile([P, 4, P], F32, tag="acc%d" % g, name="acc%d_%d_%d" % (g, q, jj))
+            for t in range(4):
+                col = (4 * g + t) * P
+                for k in (2, 1, 0):
+                    nc.tensor.matmul(acc[:, t, :], lhsT=prod[(q, k)][:, jj, col:col + P], rhs=ident_f[:],
+                                     is_transpose=True, start=(k == 2), stop=(k == 0))
+            nc.scalar.copy(out=quant[q][0][:, jj, g, :, :], in_=acc[:].rearrange("p t b -> p b t"))
 
         def quantise(q):
             grp, codes, scl = quant[q]
@@ -193,7 +188,7 @@ def tile_hiremodule_pc_kernel(tc, h_mix, w_mix, c_proj, gate_hid, wa2, ba2, wo, 
         def mx_pair(q, jj, nh):
             codes, scl = quant[q][1], quant[q][2]
             ns = slice(nh * HALF, (nh + 1) * HALF)
-            o = psum.tile([P, HALF], F32, tag="o", name="o%d_%d_%d" % (nh, q, jj), bufs=3)
+            o = psum.tile([P, HALF], F32, tag="o", name="o%d_%d_%d" % (nh, q, jj), bufs=2)
             for g in range(2):
                 gs = slice((2 * jj + g) * P, (2 * jj + g + 1) * P)
                 nc.tensor.matmul_mx(
@@ -220,21 +215,17 @@ def tile_hiremodule_pc_kernel(tc, h_mix, w_mix, c_proj, gate_hid, wa2, ba2, wo, 
                     m_gpsimd(q + 1)
                 if q >= 1:
                     quantise(q - 1)
-                pieces = list(V_PIECES) if q + 1 < NB else []
-                n_t = BLOCKS[q][1] if q < NB else 0
-                n_x = BLOCKS[q - 1][1] if q >= 1 else 0
-                for jj in range(max(n_t, n_x)):
-                    if jj < n_t:
-                        t_run(q, jj)
-                    take = 2 if jj == 0 else 1
-                    for (k, hf) in pieces[:take]:
+                if q + 1 < NB:
+                    for (k, hf) in V_PIECES:
                         m_vector(q + 1, k, hf)
-                    pieces = pieces[take:]
-                    if jj < n_x:
+                if q < NB:
+                    for jj in range(BLOCKS[q][1]):
+                        for g in range(2):
+                            t_run(q, jj, g)
+                if q >= 1:
+                    for jj in range(BLOCKS[q - 1][1]):
                         for nh in range(2):
                             add_bias(q - 1, jj, nh, mx_pair(q - 1, jj, nh))
-                for (k, hf) in pieces:
-                    m_vector(q + 1, k, hf)
                 if q + 1 < NB:
                     ij_end = BLOCKS[q + 1][0] + BLOCKS[q + 1][1]
                     for c in range(len(CHUNKS) - XBUFS):

@@ -15,9 +15,10 @@ P = 128
 B, HW, C, GH, NBR = 128, 25, 1024, 256, 3
 HALF = 512
 XBUFS = 3
-CHUNKS = ((0, 5), (5, 4), (9, 4), (13, 4), (17, 4), (21, 4))
+CHUNKS = ((0, 1), (1, 4), (5, 4), (9, 4), (13, 4), (17, 4), (21, 4))
 BLOCKS = ((0, 1),) + tuple((1 + 2 * i, 2) for i in range(11)) + ((23, 1), (24, 1))
 NB = len(BLOCKS)
+SBUF_GATE_BLOCKS = 2
 
 FLOPS = 2 * B * HW * C * C + 2 * B * GH * NBR * C
 
@@ -28,9 +29,11 @@ def tile_hiremodule_pc_kernel(tc, h_mix, w_mix, c_proj, gate_hid, wa2, ba2, wo, 
     outv = out.rearrange("b i j c -> b (i j) c")
 
     with ExitStack() as ctx:
+        ctx.enter_context(tc.manual_schedule())
         consts = ctx.enter_context(tc.tile_pool(name="consts", bufs=1))
         xpool = ctx.enter_context(tc.tile_pool(name="xpool", bufs=XBUFS))
         ppool = ctx.enter_context(tc.tile_pool(name="ppool", bufs=2))
+        gpool = ctx.enter_context(tc.tile_pool(name="gpool", bufs=2))
         psum = ctx.enter_context(tc.psum_pool(name="psum", bufs=1))
 
         ident_f = consts.tile([P, P], F32, name="ident_f")
@@ -41,6 +44,11 @@ def tile_hiremodule_pc_kernel(tc, h_mix, w_mix, c_proj, gate_hid, wa2, ba2, wo, 
         w_scales = consts.tile([P, 2, C], U8, name="w_scales", align_bytes=64)
 
         xt = {}
+        a_ps = {}
+        prod = {}
+        quant = {}
+        stage = {}
+        pools = {}
 
         def load_chunk(c):
             i0, cn = CHUNKS[c]
@@ -49,90 +57,11 @@ def tile_hiremodule_pc_kernel(tc, h_mix, w_mix, c_proj, gate_hid, wa2, ba2, wo, 
                 nc.sync.dma_start(out=t[:], in_=xv[k][:, i0:i0 + cn, :])
                 xt[(k, c)] = t
 
-        z_tags = (("pa", "pb"), ("pc", "pd"), ("o", "o"))
-        a_ps = {}
-
-        with tc.tile_pool(name="head", bufs=1) as head:
-            make_identity(nc, ident_b[:])
-            make_identity(nc, ident_f[:])
-
-            gh = head.tile([P, GH], BF16, name="gh")
-            nc.sync.dma_start(out=gh[:], in_=gate_hid)
-            ba_rows = head.tile([P, NBR * C], BF16, name="ba_rows")
-            nc.vector.memset(ba_rows[:], 0.0)
-            nc.sync.dma_start(out=ba_rows[0:1, :], in_=ba2.rearrange("(o c) -> o c", o=1))
-            wa = head.tile([P, 2, NBR * C], BF16, name="wa")
-            wav = wa2.rearrange("(kc p) c -> p kc c", p=P)
-            for hf in range(2):
-                cols = slice(hf * NBR * HALF, (hf + 1) * NBR * HALF)
-                nc.sync.dma_start(out=wa[:, :, cols], in_=wav[:, :, cols])
-            wo_raw = head.tile([P, 2, 4, C], BF16, name="wo_raw")
-            nc.sync.dma_start(out=wo_raw[:], in_=wo.rearrange("(g t p) n -> p g t n", g=2, t=4, p=P))
-            nc.sync.dma_start(out=bo_bc[:], in_=bo.partition_broadcast(P))
-            for c in range(XBUFS):
-                load_chunk(c)
-
-            ones_b = head.tile([P, P], BF16, name="ones_b")
-            nc.vector.memset(ones_b[:], 1.0)
-            warm = head.tile([P, 1], F32, name="warm")
-            nc.vector.memset(warm[:], 0.0)
-            nc.scalar.activation(out=warm[:], in_=warm[:], func=ACT.Exp)
-
-            ght_ps = psum.tile([P, 2, P], BF16, tag="acc0", name="ght_ps")
-            for kc in range(2):
-                nc.tensor.transpose(ght_ps[:, kc, :], gh[:, kc * P:(kc + 1) * P], ident_b[:])
-            ght = head.tile([P, 2, P], BF16, name="ght")
-            nc.vector.tensor_copy(out=ght[:], in_=ght_ps[:])
-
-            for hf in range(2):
-                cols = slice(hf * NBR * HALF, (hf + 1) * NBR * HALF)
-                z = []
-                for k in range(NBR):
-                    zt = psum.tile([P, HALF], F32, tag=z_tags[k][hf], name="z%d_%d" % (k, hf),
-                                   bufs=(2 if z_tags[k][hf] == "o" else 1))
-                    nc.tensor.matmul(
-                        zt[:], lhsT=ones_b[:],
-                        rhs=ba_rows[:, cols].rearrange("p (c k) -> p c k", k=NBR)[:, :, k],
-                        start=True, stop=False)
-                    for kc in range(2):
-                        nc.tensor.matmul(
-                            zt[:], lhsT=ght[:, kc, :],
-                            rhs=wa[:, kc, cols].rearrange("p (c k) -> p c k", k=NBR)[:, :, k],
-                            start=False, stop=(kc == 1))
-                    z.append(zt)
-                zs0 = head.tile([P, HALF], F32, name="zs0_%d" % hf)
-                nc.scalar.copy(out=zs0[:], in_=z[0][:])
-                m = head.tile([P, HALF], F32, name="m_%d" % hf)
-                nc.vector.tensor_tensor(out=m[:], in0=z[1][:], in1=zs0[:], op=ALU.max)
-                nc.vector.tensor_tensor(out=m[:], in0=z[2][:], in1=m[:], op=ALU.max)
-                e = head.tile([P, NBR, HALF], F32, name="e_%d" % hf)
-                for k in range(NBR):
-                    nc.vector.tensor_tensor(out=e[:, k, :], in0=z[k][:], in1=m[:], op=ALU.subtract)
-                nc.scalar.activation(out=e[:], in_=e[:], func=ACT.Exp)
-                s = head.tile([P, HALF], F32, name="s_%d" % hf)
-                nc.vector.tensor_tensor(out=s[:], in0=e[:, 0, :], in1=e[:, 1, :], op=ALU.add)
-                nc.vector.tensor_tensor(out=s[:], in0=s[:], in1=e[:, 2, :], op=ALU.add)
-                nc.vector.reciprocal(out=s[:], in_=s[:])
-                nc.vector.tensor_tensor(
-                    out=a_sb[:, :, hf * HALF:(hf + 1) * HALF], in0=e[:],
-                    in1=s[:].unsqueeze(1).to_broadcast([P, NBR, HALF]), op=ALU.mult)
-                for k in range(2):
-                    ap = psum.tile([P, HALF], F32, tag=z_tags[k][hf], name="aps%d_%d" % (k, hf))
-                    nc.tensor.matmul(ap[:], lhsT=ident_f[:], rhs=a_sb[:, k, hf * HALF:(hf + 1) * HALF],
-                                     start=True, stop=True)
-                    a_ps[(k, hf)] = ap
-
-            for g in range(2):
-                wo_grp = head.tile([P, C, 4], BF16, tag="wo_grp", name="wo_grp%d" % g, align_bytes=64)
-                for nh in range(2):
-                    ns = slice(nh * HALF, (nh + 1) * HALF)
-                    nc.scalar.copy(out=wo_grp[:, ns, :], in_=wo_raw[:, g, :, ns].rearrange("p t n -> p n t"))
-                nc.vector.quantize_mx(
-                    out=w_codes[:, g, :].bitcast(FP8X4), scales=w_scales[:, g, :],
-                    in_=wo_grp[:].rearrange("p n t -> p (n t)"))
-
-        gpool = ctx.enter_context(tc.tile_pool(name="gpool", bufs=3))
-        opool = ctx.enter_context(tc.tile_pool(name="opool", bufs=3))
+        def load_after(q):
+            ij_end = BLOCKS[q][0] + BLOCKS[q][1]
+            for c in range(len(CHUNKS) - XBUFS):
+                if CHUNKS[c][0] + CHUNKS[c][1] == ij_end:
+                    load_chunk(c + XBUFS)
 
         def where(ij):
             for c in range(len(CHUNKS)):
@@ -141,41 +70,56 @@ def tile_hiremodule_pc_kernel(tc, h_mix, w_mix, c_proj, gate_hid, wa2, ba2, wo, 
                     return c, ij - i0
             return None
 
-        prod = {}
-        quant = {}
-        stage = {}
-
-        def m_gpsimd(q):
-            ij0, n = BLOCKS[q]
-            c, j0 = where(ij0)
+        def new_products(q):
+            n = BLOCKS[q][1]
             for k in range(NBR):
                 prod[(q, k)] = ppool.tile([P, n, C], F32, tag="p%d" % k, name="p%d_%d" % (k, q))
+
+        def m_gpsimd(q, k, lo, hi, j_lo, j_hi):
+            c, j0 = where(BLOCKS[q][0])
             nc.gpsimd.tensor_tensor(
-                out=prod[(q, 2)][:], in0=xt[(2, c)][:, j0:j0 + n, :],
-                in1=a_sb[:, 2, :].unsqueeze(1).to_broadcast([P, n, C]), op=ALU.mult)
+                out=prod[(q, k)][:, j_lo:j_hi, lo:hi], in0=xt[(k, c)][:, j0 + j_lo:j0 + j_hi, lo:hi],
+                in1=a_sb[:, k, lo:hi].unsqueeze(1).to_broadcast([P, j_hi - j_lo, hi - lo]), op=ALU.mult)
 
-        def m_vector(q, k, hf):
-            ij0, n = BLOCKS[q]
-            c, j0 = where(ij0)
+        def m_vector(q, k, hf, j_lo, j_hi):
+            c, j0 = where(BLOCKS[q][0])
             hs = slice(hf * HALF, (hf + 1) * HALF)
+            gate = a_ps[(k, hf)][:] if (q >= SBUF_GATE_BLOCKS and (k, hf) in a_ps) else a_sb[:, k, hs]
             nc.vector.tensor_tensor(
-                out=prod[(q, k)][:, :, hs], in0=xt[(k, c)][:, j0:j0 + n, hs],
-                in1=a_ps[(k, hf)][:].unsqueeze(1).to_broadcast([P, n, HALF]), op=ALU.mult)
+                out=prod[(q, k)][:, j_lo:j_hi, hs], in0=xt[(k, c)][:, j0 + j_lo:j0 + j_hi, hs],
+                in1=gate.unsqueeze(1).to_broadcast([P, j_hi - j_lo, HALF]), op=ALU.mult)
 
-        V_PIECES = ((0, 1), (0, 0), (1, 1), (1, 0))
+        def pre_add(q):
+            nc.vector.tensor_tensor(out=prod[(q, 0)][:, :, 0:HALF], in0=prod[(q, 0)][:, :, 0:HALF],
+                                    in1=prod[(q, 1)][:, :, 0:HALF], op=ALU.add)
+
+        def gpsimd_share(q):
+            n = BLOCKS[q][1]
+            if n == 2:
+                m_gpsimd(q, 1, HALF, C, 1, 2)
+            m_gpsimd(q, 2, 0, C, 0, n)
+
+        def vector_share(q):
+            n = BLOCKS[q][1]
+            m_vector(q, 0, 1, 0, n)
+            m_vector(q, 1, 1, 0, 1)
+            m_vector(q, 0, 0, 0, n)
+            m_vector(q, 1, 0, 0, n)
+            pre_add(q)
 
         def t_run(q, jj, g):
             n = BLOCKS[q][1]
-            if (jj, g) == (0, 0):
+            if q not in quant:
                 quant[q] = (
                     gpool.tile([P, n, 2, P, 4], BF16, tag="grp", name="grp%d" % q, align_bytes=64),
                     gpool.tile([P, n * 2 * P], U32, tag="codes", name="codes%d" % q, align_bytes=64),
                     gpool.tile([P, n * 2 * P], U8, tag="scl", name="scl%d" % q, align_bytes=64),
                 )
-            acc = psum.tile([P, 4, P], F32, tag="acc%d" % g, name="acc%d_%d_%d" % (g, q, jj))
+            acc = psum.tile([P, 4, P], F32, tag="acc", name="acc%d_%d_%d" % (g, q, jj), bufs=2)
+            srcs = (2, 0) if g == 0 else (2, 1, 0)
             for t in range(4):
                 col = (4 * g + t) * P
-                for k in (2, 1, 0):
+                for k in srcs:
                     nc.tensor.matmul(acc[:, t, :], lhsT=prod[(q, k)][:, jj, col:col + P], rhs=ident_f[:],
                                      is_transpose=True, start=(k == 2), stop=(k == 0))
             nc.scalar.copy(out=quant[q][0][:, jj, g, :, :], in_=acc[:].rearrange("p t b -> p b t"))
@@ -188,7 +132,7 @@ def tile_hiremodule_pc_kernel(tc, h_mix, w_mix, c_proj, gate_hid, wa2, ba2, wo, 
         def mx_pair(q, jj, nh):
             codes, scl = quant[q][1], quant[q][2]
             ns = slice(nh * HALF, (nh + 1) * HALF)
-            o = psum.tile([P, HALF], F32, tag="o", name="o%d_%d_%d" % (nh, q, jj), bufs=2)
+            o = psum.tile([P, HALF], F32, tag="o", name="o%d_%d_%d" % (nh, q, jj), bufs=3)
             for g in range(2):
                 gs = slice((2 * jj + g) * P, (2 * jj + g + 1) * P)
                 nc.tensor.matmul_mx(
@@ -200,34 +144,149 @@ def tile_hiremodule_pc_kernel(tc, h_mix, w_mix, c_proj, gate_hid, wa2, ba2, wo, 
         def add_bias(q, jj, nh, o):
             ij0, n = BLOCKS[q]
             if (jj, nh) == (0, 0):
-                stage[q] = opool.tile([P, n, C], F32, tag="ost", name="ost%d" % q)
+                stage[q] = pools["o"].tile([P, n, C], F32, tag="ost", name="ost%d" % q)
             ns = slice(nh * HALF, (nh + 1) * HALF)
             nc.vector.tensor_tensor(out=stage[q][:, jj, ns], in0=o[:], in1=bo_bc[:, ns], op=ALU.add)
             if (jj, nh) == (n - 1, 1):
                 nc.sync.dma_start(out=outv[:, ij0:ij0 + n, :], in_=stage[q][:])
 
-        with tc.manual_schedule():
-            m_gpsimd(0)
-            for (k, hf) in V_PIECES:
-                m_vector(0, k, hf)
-            for q in range(NB + 1):
-                if q + 1 < NB:
-                    m_gpsimd(q + 1)
-                if q >= 1:
-                    quantise(q - 1)
-                if q + 1 < NB:
-                    for (k, hf) in V_PIECES:
-                        m_vector(q + 1, k, hf)
-                if q < NB:
-                    for jj in range(BLOCKS[q][1]):
-                        for g in range(2):
-                            t_run(q, jj, g)
-                if q >= 1:
-                    for jj in range(BLOCKS[q - 1][1]):
-                        for nh in range(2):
-                            add_bias(q - 1, jj, nh, mx_pair(q - 1, jj, nh))
-                if q + 1 < NB:
-                    ij_end = BLOCKS[q + 1][0] + BLOCKS[q + 1][1]
-                    for c in range(len(CHUNKS) - XBUFS):
-                        if CHUNKS[c][0] + CHUNKS[c][1] == ij_end:
-                            load_chunk(c + XBUFS)
+        z_tags = (("pa", "pb"), ("pc", "o"), ("o", "o"))
+
+        with tc.tile_pool(name="head", bufs=1) as head:
+            make_identity(nc, ident_b[:])
+            make_identity(nc, ident_f[:])
+
+            ba_rows = head.tile([P, NBR * C], BF16, name="ba_rows")
+            nc.vector.memset(ba_rows[:], 0.0)
+            ones_b = head.tile([P, P], BF16, name="ones_b")
+            nc.vector.memset(ones_b[:], 1.0)
+            warm = head.tile([P, 1], F32, name="warm")
+            nc.vector.memset(warm[:], 0.0)
+
+            gh = head.tile([P, GH], BF16, name="gh")
+            nc.sync.dma_start(out=gh[:], in_=gate_hid)
+            nc.sync.dma_start(out=ba_rows[0:1, :], in_=ba2.rearrange("(o c) -> o c", o=1))
+            wa = head.tile([P, 2, NBR * C], BF16, tag="wa", name="wa", align_bytes=64)
+            wav = wa2.rearrange("(kc p) c -> p kc c", p=P)
+            for hf in range(2):
+                cols = slice(hf * NBR * HALF, (hf + 1) * NBR * HALF)
+                nc.sync.dma_start(out=wa[:, :, cols], in_=wav[:, :, cols])
+            load_chunk(0)
+            wo_raw = head.tile([P, 2, 4, C], BF16, name="wo_raw")
+            nc.sync.dma_start(out=wo_raw[:], in_=wo.rearrange("(g t p) n -> p g t n", g=2, t=4, p=P))
+            load_chunk(1)
+            load_chunk(2)
+            nc.sync.dma_start(out=bo_bc[:], in_=bo.partition_broadcast(P))
+
+            nc.scalar.activation(out=warm[:], in_=warm[:], func=ACT.Exp)
+
+            ght_ps = psum.tile([P, 2, P], BF16, tag="acc", name="ght_ps", bufs=2)
+            for kc in range(2):
+                nc.tensor.transpose(ght_ps[:, kc, :], gh[:, kc * P:(kc + 1) * P], ident_b[:])
+            ght = head.tile([P, 2, P], BF16, name="ght")
+            nc.vector.tensor_copy(out=ght[:], in_=ght_ps[:])
+
+            z = {}
+            for hf in range(2):
+                cols = slice(hf * NBR * HALF, (hf + 1) * NBR * HALF)
+                for k in range(NBR):
+                    zt = psum.tile([P, HALF], F32, tag=z_tags[k][hf], name="z%d_%d" % (k, hf),
+                                   bufs=(3 if z_tags[k][hf] == "o" else 1))
+                    nc.tensor.matmul(
+                        zt[:], lhsT=ones_b[:],
+                        rhs=ba_rows[:, cols].rearrange("p (c k) -> p c k", k=NBR)[:, :, k],
+                        start=True, stop=False)
+                    z[(k, hf)] = zt
+                for k in range(NBR):
+                    for kc in range(2):
+                        nc.tensor.matmul(
+                            z[(k, hf)][:], lhsT=ght[:, kc, :],
+                            rhs=wa[:, kc, cols].rearrange("p (c k) -> p c k", k=NBR)[:, :, k],
+                            start=False, stop=(kc == 1))
+
+            e = {}
+            s = {}
+            mx = {}
+            for hf in range(2):
+                mx[hf] = head.tile([P, HALF], F32, name="m_%d" % hf)
+                nc.scalar.copy(out=mx[hf][:], in_=z[(0, hf)][:])
+            for hf in range(2):
+                m = mx[hf]
+                nc.vector.tensor_tensor(out=m[:], in0=z[(1, hf)][:], in1=m[:], op=ALU.max)
+                nc.vector.tensor_tensor(out=m[:], in0=z[(2, hf)][:], in1=m[:], op=ALU.max)
+                e[hf] = head.tile([P, NBR, HALF], F32, name="e_%d" % hf)
+                for k in range(NBR):
+                    nc.vector.tensor_tensor(out=e[hf][:, k, :], in0=z[(k, hf)][:], in1=m[:], op=ALU.subtract)
+                nc.scalar.activation(out=e[hf][:], in_=e[hf][:], func=ACT.Exp)
+
+            wo_grp = [head.tile([P, C, 4], BF16, tag="wa", name="wo_grp0", align_bytes=64),
+                      head.tile([P, C, 4], BF16, name="wo_grp1", align_bytes=64)]
+            for nh in range(2):
+                ns = slice(nh * HALF, (nh + 1) * HALF)
+                nc.gpsimd.tensor_scalar(out=wo_grp[0][:, ns, :],
+                                        in0=wo_raw[:, 0, :, ns].rearrange("p t n -> p n t"),
+                                        scalar1=1.0, scalar2=0.0, op0=ALU.mult, op1=ALU.add)
+
+            y = {}
+            for hf in range(2):
+                s[hf] = head.tile([P, HALF], F32, name="s_%d" % hf)
+                y[hf] = head.tile([P, HALF], F32, name="y_%d" % hf)
+                nc.vector.tensor_tensor(out=s[hf][:], in0=e[hf][:, 0, :], in1=e[hf][:, 1, :], op=ALU.add)
+                nc.vector.tensor_tensor(out=s[hf][:], in0=s[hf][:], in1=e[hf][:, 2, :], op=ALU.add)
+            for hf in range(2):
+                nc.scalar.activation(out=y[hf][:], in_=s[hf][:], func=ACT.Abs_reciprocal_sqrt)
+                nc.scalar.activation(out=y[hf][:], in_=y[hf][:], func=ACT.Square)
+            nc.vector.tensor_copy(out=wo_grp[1][:], in_=wo_raw[:, 1, :, :].rearrange("p t n -> p n t"))
+
+            new_products(0)
+            for hf in range(2):
+                hs = slice(hf * HALF, (hf + 1) * HALF)
+                nc.vector.tensor_tensor(out=s[hf][:], in0=s[hf][:], in1=y[hf][:], op=ALU.mult)
+                nc.vector.scalar_tensor_tensor(out=y[hf][:], in0=s[hf][:], scalar=2.0, in1=y[hf][:],
+                                               op0=ALU.subtract, op1=ALU.mult)
+                nc.vector.scalar_tensor_tensor(
+                    out=a_sb[:, :, hs], in0=e[hf][:], scalar=-1.0,
+                    in1=y[hf][:].unsqueeze(1).to_broadcast([P, NBR, HALF]), op0=ALU.mult, op1=ALU.mult)
+                m_gpsimd(0, 2, hf * HALF, (hf + 1) * HALF, 0, 1)
+                m_vector(0, 0, hf, 0, 1)
+                m_vector(0, 1, hf, 0, 1)
+                if hf == 0:
+                    pre_add(0)
+            load_after(0)
+
+            def gate_to_psum(k, hf):
+                ap = psum.tile([P, HALF], F32, tag=z_tags[k][hf], name="aps%d_%d" % (k, hf))
+                nc.tensor.matmul(ap[:], lhsT=ident_f[:], rhs=a_sb[:, k, hf * HALF:(hf + 1) * HALF],
+                                 start=True, stop=True)
+                a_ps[(k, hf)] = ap
+
+            new_products(1)
+            gpsimd_share(1)
+            vector_share(1)
+            load_after(1)
+            t_run(0, 0, 0)
+            gate_to_psum(0, 0)
+            gate_to_psum(1, 0)
+            t_run(0, 0, 1)
+            gate_to_psum(0, 1)
+            for g in range(2):
+                nc.vector.quantize_mx(out=w_codes[:, g, :].bitcast(FP8X4), scales=w_scales[:, g, :],
+                                      in_=wo_grp[g][:].rearrange("p n t -> p (n t)"))
+
+        pools["o"] = ctx.enter_context(tc.tile_pool(name="opool", bufs=3))
+
+        for q in range(1, NB + 1):
+            if q + 1 < NB:
+                new_products(q + 1)
+                gpsimd_share(q + 1)
+            quantise(q - 1)
+            if q + 1 < NB:
+                vector_share(q + 1)
+                load_after(q + 1)
+            if q < NB:
+                for jj in range(BLOCKS[q][1]):
+                    for g in range(2):
+                        t_run(q, jj, g)
+            for jj in range(BLOCKS[q - 1][1]):
+                for nh in range(2):
+                    add_bias(q - 1, jj, nh, mx_pair(q - 1, jj, nh))

@@ -18,7 +18,6 @@ XBUFS = 3
 CHUNKS = ((0, 1), (1, 4), (5, 4), (9, 4), (13, 4), (17, 4), (21, 4))
 BLOCKS = ((0, 1),) + tuple((1 + 2 * i, 2) for i in range(11)) + ((23, 1), (24, 1))
 NB = len(BLOCKS)
-SBUF_GATE_BLOCKS = 2
 
 FLOPS = 2 * B * HW * C * C + 2 * B * GH * NBR * C
 
@@ -75,37 +74,34 @@ def tile_hiremodule_pc_kernel(tc, h_mix, w_mix, c_proj, gate_hid, wa2, ba2, wo, 
             for k in range(NBR):
                 prod[(q, k)] = ppool.tile([P, n, C], F32, tag="p%d" % k, name="p%d_%d" % (k, q))
 
-        def m_gpsimd(q, k, lo, hi, j_lo, j_hi):
-            c, j0 = where(BLOCKS[q][0])
-            nc.gpsimd.tensor_tensor(
-                out=prod[(q, k)][:, j_lo:j_hi, lo:hi], in0=xt[(k, c)][:, j0 + j_lo:j0 + j_hi, lo:hi],
-                in1=a_sb[:, k, lo:hi].unsqueeze(1).to_broadcast([P, j_hi - j_lo, hi - lo]), op=ALU.mult)
+        def pre_added(q):
+            return BLOCKS[q][1] == 2
 
-        def m_vector(q, k, hf, j_lo, j_hi):
-            c, j0 = where(BLOCKS[q][0])
-            hs = slice(hf * HALF, (hf + 1) * HALF)
-            gate = a_ps[(k, hf)][:] if (q >= SBUF_GATE_BLOCKS and (k, hf) in a_ps) else a_sb[:, k, hs]
-            nc.vector.tensor_tensor(
-                out=prod[(q, k)][:, j_lo:j_hi, hs], in0=xt[(k, c)][:, j0 + j_lo:j0 + j_hi, hs],
-                in1=gate.unsqueeze(1).to_broadcast([P, j_hi - j_lo, HALF]), op=ALU.mult)
-
-        def pre_add(q):
-            nc.vector.tensor_tensor(out=prod[(q, 0)][:, :, 0:HALF], in0=prod[(q, 0)][:, :, 0:HALF],
-                                    in1=prod[(q, 1)][:, :, 0:HALF], op=ALU.add)
+        def touch(q):
+            nc.vector.memset(prod[(q, 2)][:, 0, 0:8], 0.0)
 
         def gpsimd_share(q):
             n = BLOCKS[q][1]
-            if n == 2:
-                m_gpsimd(q, 1, HALF, C, 1, 2)
-            m_gpsimd(q, 2, 0, C, 0, n)
+            c, j0 = where(BLOCKS[q][0])
+            for hf in range(2):
+                hs = slice(hf * HALF, (hf + 1) * HALF)
+                nc.gpsimd.tensor_tensor(
+                    out=prod[(q, 2)][:, :, hs], in0=xt[(2, c)][:, j0:j0 + n, hs],
+                    in1=a_sb[:, 2, hs].unsqueeze(1).to_broadcast([P, n, HALF]), op=ALU.mult)
+
+        def gpsimd_add(q):
+            if pre_added(q):
+                nc.gpsimd.tensor_tensor(out=prod[(q, 2)][:, :, 0:HALF], in0=prod[(q, 2)][:, :, 0:HALF],
+                                        in1=prod[(q, 1)][:, :, 0:HALF], op=ALU.add)
 
         def vector_share(q):
             n = BLOCKS[q][1]
-            m_vector(q, 0, 1, 0, n)
-            m_vector(q, 1, 1, 0, 1)
-            m_vector(q, 0, 0, 0, n)
-            m_vector(q, 1, 0, 0, n)
-            pre_add(q)
+            c, j0 = where(BLOCKS[q][0])
+            for (k, hf) in ((1, 0), (0, 0), (0, 1), (1, 1)):
+                hs = slice(hf * HALF, (hf + 1) * HALF)
+                nc.vector.tensor_tensor(
+                    out=prod[(q, k)][:, :, hs], in0=xt[(k, c)][:, j0:j0 + n, hs],
+                    in1=a_ps[(k, hf)][:].unsqueeze(1).to_broadcast([P, n, HALF]), op=ALU.mult)
 
         def t_run(q, jj, g):
             n = BLOCKS[q][1]
@@ -116,7 +112,7 @@ def tile_hiremodule_pc_kernel(tc, h_mix, w_mix, c_proj, gate_hid, wa2, ba2, wo, 
                     gpool.tile([P, n * 2 * P], U8, tag="scl", name="scl%d" % q, align_bytes=64),
                 )
             acc = psum.tile([P, 4, P], F32, tag="acc", name="acc%d_%d_%d" % (g, q, jj), bufs=2)
-            srcs = (2, 0) if g == 0 else (2, 1, 0)
+            srcs = (2, 0) if (g == 0 and pre_added(q)) else (2, 1, 0)
             for t in range(4):
                 col = (4 * g + t) * P
                 for k in srcs:
@@ -132,7 +128,7 @@ def tile_hiremodule_pc_kernel(tc, h_mix, w_mix, c_proj, gate_hid, wa2, ba2, wo, 
         def mx_pair(q, jj, nh):
             codes, scl = quant[q][1], quant[q][2]
             ns = slice(nh * HALF, (nh + 1) * HALF)
-            o = psum.tile([P, HALF], F32, tag="o", name="o%d_%d_%d" % (nh, q, jj), bufs=3)
+            o = psum.tile([P, HALF], F32, tag="o", name="o%d_%d_%d" % (nh, q, jj), bufs=2)
             for g in range(2):
                 gs = slice((2 * jj + g) * P, (2 * jj + g + 1) * P)
                 nc.tensor.matmul_mx(
@@ -150,7 +146,7 @@ def tile_hiremodule_pc_kernel(tc, h_mix, w_mix, c_proj, gate_hid, wa2, ba2, wo, 
             if (jj, nh) == (n - 1, 1):
                 nc.sync.dma_start(out=outv[:, ij0:ij0 + n, :], in_=stage[q][:])
 
-        z_tags = (("pa", "pb"), ("pc", "o"), ("o", "o"))
+        z_tags = (("pa", "pb"), ("pc", "pd"), ("o", "o"))
 
         with tc.tile_pool(name="head", bufs=1) as head:
             make_identity(nc, ident_b[:])
@@ -171,11 +167,10 @@ def tile_hiremodule_pc_kernel(tc, h_mix, w_mix, c_proj, gate_hid, wa2, ba2, wo, 
             for hf in range(2):
                 cols = slice(hf * NBR * HALF, (hf + 1) * NBR * HALF)
                 nc.sync.dma_start(out=wa[:, :, cols], in_=wav[:, :, cols])
-            load_chunk(0)
             wo_raw = head.tile([P, 2, 4, C], BF16, name="wo_raw")
             nc.sync.dma_start(out=wo_raw[:], in_=wo.rearrange("(g t p) n -> p g t n", g=2, t=4, p=P))
-            load_chunk(1)
-            load_chunk(2)
+            for c in range(XBUFS):
+                load_chunk(c)
             nc.sync.dma_start(out=bo_bc[:], in_=bo.partition_broadcast(P))
 
             nc.scalar.activation(out=warm[:], in_=warm[:], func=ACT.Exp)
@@ -191,7 +186,7 @@ def tile_hiremodule_pc_kernel(tc, h_mix, w_mix, c_proj, gate_hid, wa2, ba2, wo, 
                 cols = slice(hf * NBR * HALF, (hf + 1) * NBR * HALF)
                 for k in range(NBR):
                     zt = psum.tile([P, HALF], F32, tag=z_tags[k][hf], name="z%d_%d" % (k, hf),
-                                   bufs=(3 if z_tags[k][hf] == "o" else 1))
+                                   bufs=(2 if z_tags[k][hf] == "o" else 1))
                     nc.tensor.matmul(
                         zt[:], lhsT=ones_b[:],
                         rhs=ba_rows[:, cols].rearrange("p (c k) -> p c k", k=NBR)[:, :, k],
@@ -204,8 +199,17 @@ def tile_hiremodule_pc_kernel(tc, h_mix, w_mix, c_proj, gate_hid, wa2, ba2, wo, 
                             rhs=wa[:, kc, cols].rearrange("p (c k) -> p c k", k=NBR)[:, :, k],
                             start=False, stop=(kc == 1))
 
+            wo_grp = [head.tile([P, C, 4], BF16, tag="wa", name="wo_grp0", align_bytes=64),
+                      head.tile([P, C, 4], BF16, name="wo_grp1", align_bytes=64)]
+            for piece in range(4):
+                ns = slice(piece * 256, (piece + 1) * 256)
+                nc.gpsimd.tensor_scalar(out=wo_grp[1][:, ns, :],
+                                        in0=wo_raw[:, 1, :, ns].rearrange("p t n -> p n t"),
+                                        scalar1=1.0, scalar2=0.0, op0=ALU.mult, op1=ALU.add)
+
             e = {}
             s = {}
+            y = {}
             mx = {}
             for hf in range(2):
                 mx[hf] = head.tile([P, HALF], F32, name="m_%d" % hf)
@@ -218,16 +222,6 @@ def tile_hiremodule_pc_kernel(tc, h_mix, w_mix, c_proj, gate_hid, wa2, ba2, wo, 
                 for k in range(NBR):
                     nc.vector.tensor_tensor(out=e[hf][:, k, :], in0=z[(k, hf)][:], in1=m[:], op=ALU.subtract)
                 nc.scalar.activation(out=e[hf][:], in_=e[hf][:], func=ACT.Exp)
-
-            wo_grp = [head.tile([P, C, 4], BF16, tag="wa", name="wo_grp0", align_bytes=64),
-                      head.tile([P, C, 4], BF16, name="wo_grp1", align_bytes=64)]
-            for nh in range(2):
-                ns = slice(nh * HALF, (nh + 1) * HALF)
-                nc.gpsimd.tensor_scalar(out=wo_grp[0][:, ns, :],
-                                        in0=wo_raw[:, 0, :, ns].rearrange("p t n -> p n t"),
-                                        scalar1=1.0, scalar2=0.0, op0=ALU.mult, op1=ALU.add)
-
-            y = {}
             for hf in range(2):
                 s[hf] = head.tile([P, HALF], F32, name="s_%d" % hf)
                 y[hf] = head.tile([P, HALF], F32, name="y_%d" % hf)
@@ -236,9 +230,12 @@ def tile_hiremodule_pc_kernel(tc, h_mix, w_mix, c_proj, gate_hid, wa2, ba2, wo, 
             for hf in range(2):
                 nc.scalar.activation(out=y[hf][:], in_=s[hf][:], func=ACT.Abs_reciprocal_sqrt)
                 nc.scalar.activation(out=y[hf][:], in_=y[hf][:], func=ACT.Square)
-            nc.vector.tensor_copy(out=wo_grp[1][:], in_=wo_raw[:, 1, :, :].rearrange("p t n -> p n t"))
+            nc.vector.quantize_mx(out=w_codes[:, 1, :].bitcast(FP8X4), scales=w_scales[:, 1, :],
+                                  in_=wo_grp[1][:].rearrange("p n t -> p (n t)"))
+            for piece in range(4):
+                ns = slice(piece * 256, (piece + 1) * 256)
+                nc.scalar.copy(out=wo_grp[0][:, ns, :], in_=wo_raw[:, 0, :, ns].rearrange("p t n -> p n t"))
 
-            new_products(0)
             for hf in range(2):
                 hs = slice(hf * HALF, (hf + 1) * HALF)
                 nc.vector.tensor_tensor(out=s[hf][:], in0=s[hf][:], in1=y[hf][:], op=ALU.mult)
@@ -247,46 +244,40 @@ def tile_hiremodule_pc_kernel(tc, h_mix, w_mix, c_proj, gate_hid, wa2, ba2, wo, 
                 nc.vector.scalar_tensor_tensor(
                     out=a_sb[:, :, hs], in0=e[hf][:], scalar=-1.0,
                     in1=y[hf][:].unsqueeze(1).to_broadcast([P, NBR, HALF]), op0=ALU.mult, op1=ALU.mult)
-                m_gpsimd(0, 2, hf * HALF, (hf + 1) * HALF, 0, 1)
-                m_vector(0, 0, hf, 0, 1)
-                m_vector(0, 1, hf, 0, 1)
-                if hf == 0:
-                    pre_add(0)
-            load_after(0)
+                for k in (1, 0):
+                    ap = psum.tile([P, HALF], F32, tag=z_tags[k][hf], name="aps%d_%d" % (k, hf))
+                    nc.tensor.matmul(ap[:], lhsT=ident_f[:], rhs=a_sb[:, k, hs], start=True, stop=True)
+                    a_ps[(k, hf)] = ap
 
-            def gate_to_psum(k, hf):
-                ap = psum.tile([P, HALF], F32, tag=z_tags[k][hf], name="aps%d_%d" % (k, hf))
-                nc.tensor.matmul(ap[:], lhsT=ident_f[:], rhs=a_sb[:, k, hf * HALF:(hf + 1) * HALF],
-                                 start=True, stop=True)
-                a_ps[(k, hf)] = ap
-
-            new_products(1)
-            gpsimd_share(1)
-            vector_share(1)
-            load_after(1)
-            t_run(0, 0, 0)
-            gate_to_psum(0, 0)
-            gate_to_psum(1, 0)
-            t_run(0, 0, 1)
-            gate_to_psum(0, 1)
-            for g in range(2):
-                nc.vector.quantize_mx(out=w_codes[:, g, :].bitcast(FP8X4), scales=w_scales[:, g, :],
-                                      in_=wo_grp[g][:].rearrange("p n t -> p (n t)"))
+            for q in range(2):
+                new_products(q)
+                gpsimd_share(q)
+            for q in range(2):
+                vector_share(q)
+                gpsimd_add(q)
+                load_after(q)
+            nc.vector.quantize_mx(out=w_codes[:, 0, :].bitcast(FP8X4), scales=w_scales[:, 0, :],
+                                  in_=wo_grp[0][:].rearrange("p n t -> p (n t)"))
 
         pools["o"] = ctx.enter_context(tc.tile_pool(name="opool", bufs=3))
 
-        for q in range(1, NB + 1):
-            if q + 1 < NB:
-                new_products(q + 1)
-                gpsimd_share(q + 1)
-            quantise(q - 1)
-            if q + 1 < NB:
-                vector_share(q + 1)
-                load_after(q + 1)
+        for q in range(NB + 1):
             if q < NB:
                 for jj in range(BLOCKS[q][1]):
                     for g in range(2):
                         t_run(q, jj, g)
-            for jj in range(BLOCKS[q - 1][1]):
-                for nh in range(2):
-                    add_bias(q - 1, jj, nh, mx_pair(q - 1, jj, nh))
+            pairs = [(jj, nh) for jj in range(BLOCKS[q - 1][1]) for nh in range(2)] if q >= 1 else []
+            for (jj, nh) in pairs[:2]:
+                add_bias(q - 1, jj, nh, mx_pair(q - 1, jj, nh))
+            if q < NB:
+                quantise(q)
+            if q + 2 < NB:
+                new_products(q + 2)
+                touch(q + 2)
+                gpsimd_share(q + 2)
+            for (jj, nh) in pairs[2:]:
+                add_bias(q - 1, jj, nh, mx_pair(q - 1, jj, nh))
+            if q + 2 < NB:
+                vector_share(q + 2)
+                gpsimd_add(q + 2)
+                load_after(q + 2)

@@ -15,8 +15,8 @@ P = 128
 B, HW, C, GH, NBR = 128, 25, 1024, 256, 3
 HALF = 512
 XBUFS = 3
-CHUNKS = ((0, 1), (1, 4), (5, 4), (9, 4), (13, 4), (17, 4), (21, 4))
-BLOCKS = ((0, 1),) + tuple((1 + 2 * i, 2) for i in range(11)) + ((23, 1), (24, 1))
+CHUNKS = ((0, 2), (2, 4), (6, 4), (10, 4), (14, 4), (18, 4), (22, 3))
+BLOCKS = ((0, 1), (1, 1)) + tuple((2 + 2 * i, 2) for i in range(11)) + ((24, 1),)
 NB = len(BLOCKS)
 
 FLOPS = 2 * B * HW * C * C + 2 * B * GH * NBR * C
@@ -77,13 +77,17 @@ def tile_hiremodule_pc_kernel(tc, h_mix, w_mix, c_proj, gate_hid, wa2, ba2, wo, 
         def pre_added(q):
             return BLOCKS[q][1] == 2
 
+        def halves(q):
+            return (1, 0) if pre_added(q) else (0, 1)
+
         def touch(q):
-            nc.vector.memset(prod[(q, 2)][:, 0, 0:8], 0.0)
+            first = halves(q)[0] * HALF
+            nc.vector.memset(prod[(q, 2)][:, 0, first:first + 8], 0.0)
 
         def gpsimd_share(q):
             n = BLOCKS[q][1]
             c, j0 = where(BLOCKS[q][0])
-            for hf in range(2):
+            for hf in halves(q):
                 hs = slice(hf * HALF, (hf + 1) * HALF)
                 nc.gpsimd.tensor_tensor(
                     out=prod[(q, 2)][:, :, hs], in0=xt[(2, c)][:, j0:j0 + n, hs],
@@ -97,7 +101,7 @@ def tile_hiremodule_pc_kernel(tc, h_mix, w_mix, c_proj, gate_hid, wa2, ba2, wo, 
         def vector_share(q):
             n = BLOCKS[q][1]
             c, j0 = where(BLOCKS[q][0])
-            for (k, hf) in ((1, 0), (0, 0), (0, 1), (1, 1)):
+            for (k, hf) in [(k, hf) for hf in halves(q) for k in (1, 0)]:
                 hs = slice(hf * HALF, (hf + 1) * HALF)
                 nc.vector.tensor_tensor(
                     out=prod[(q, k)][:, :, hs], in0=xt[(k, c)][:, j0:j0 + n, hs],
@@ -263,8 +267,8 @@ def tile_hiremodule_pc_kernel(tc, h_mix, w_mix, c_proj, gate_hid, wa2, ba2, wo, 
 
         for q in range(NB + 1):
             if q < NB:
-                for jj in range(BLOCKS[q][1]):
-                    for g in range(2):
+                for g in halves(q):
+                    for jj in range(BLOCKS[q][1]):
                         t_run(q, jj, g)
             pairs = [(jj, nh) for jj in range(BLOCKS[q - 1][1]) for nh in range(2)] if q >= 1 else []
             for (jj, nh) in pairs[:2]:

from contextlib import ExitStack

import concourse.mybir as mybir
from concourse.masks import make_identity

F32 = mybir.dt.float32
BF16 = mybir.dt.bfloat16
U32 = mybir.dt.uint32
U8 = mybir.dt.uint8
FP8X4 = mybir.dt.float8_e4m3fn_x4
ALU = mybir.AluOpType
ACT = mybir.ActivationFunctionType

P = 128
B, HW, C, GH, NBR = 128, 25, 1024, 256, 3
HALF = 512
XBUFS = 3
CHUNKS = ((0, 2), (2, 4), (6, 4), (10, 4), (14, 4), (18, 4), (22, 3))
BLOCKS = ((0, 1), (1, 1)) + tuple((2 + 2 * i, 2) for i in range(11)) + ((24, 1),)
NB = len(BLOCKS)

FLOPS = 2 * B * HW * C * C + 2 * B * GH * NBR * C


def tile_hiremodule_pc_kernel(tc, h_mix, w_mix, c_proj, gate_hid, wa2, ba2, wo, bo, out):
    nc = tc.nc
    xv = [x.rearrange("b i j c -> b (i j) c") for x in (h_mix, w_mix, c_proj)]
    outv = out.rearrange("b i j c -> b (i j) c")

    with ExitStack() as ctx:
        ctx.enter_context(tc.manual_schedule())
        consts = ctx.enter_context(tc.tile_pool(name="consts", bufs=1))
        xpool = ctx.enter_context(tc.tile_pool(name="xpool", bufs=XBUFS))
        ppool = ctx.enter_context(tc.tile_pool(name="ppool", bufs=2))
        gpool = ctx.enter_context(tc.tile_pool(name="gpool", bufs=2))
        psum = ctx.enter_context(tc.psum_pool(name="psum", bufs=1))

        ident_f = consts.tile([P, P], F32, name="ident_f")
        ident_b = consts.tile([P, P], BF16, name="ident_b")
        a_sb = consts.tile([P, NBR, C], F32, name="a_sb")
        bo_bc = consts.tile([P, C], BF16, name="bo_bc")
        w_codes = consts.tile([P, 2, C], U32, name="w_codes", align_bytes=64)
        w_scales = consts.tile([P, 2, C], U8, name="w_scales", align_bytes=64)

        xt = {}
        a_ps = {}
        prod = {}
        quant = {}
        stage = {}
        pools = {}

        def load_chunk(c):
            i0, cn = CHUNKS[c]
            for k in range(NBR):
                t = xpool.tile([P, cn, C], BF16, tag="x%d" % k, name="x%d_%d" % (k, c))
                nc.sync.dma_start(out=t[:], in_=xv[k][:, i0:i0 + cn, :])
                xt[(k, c)] = t

        def load_after(q):
            ij_end = BLOCKS[q][0] + BLOCKS[q][1]
            for c in range(len(CHUNKS) - XBUFS):
                if CHUNKS[c][0] + CHUNKS[c][1] == ij_end:
                    load_chunk(c + XBUFS)

        def where(ij):
            for c in range(len(CHUNKS)):
                i0, cn = CHUNKS[c]
                if i0 <= ij < i0 + cn:
                    return c, ij - i0
            return None

        def new_products(q):
            n = BLOCKS[q][1]
            for k in range(NBR):
                prod[(q, k)] = ppool.tile([P, n, C], F32, tag="p%d" % k, name="p%d_%d" % (k, q))

        def pre_added(q):
            return BLOCKS[q][1] == 2

        def halves(q):
            return (1, 0) if pre_added(q) else (0, 1)

        def touch(q):
            first = halves(q)[0] * HALF
            nc.vector.memset(prod[(q, 2)][:, 0, first:first + 8], 0.0)

        def gpsimd_share(q):
            n = BLOCKS[q][1]
            c, j0 = where(BLOCKS[q][0])
            for hf in halves(q):
                hs = slice(hf * HALF, (hf + 1) * HALF)
                nc.gpsimd.tensor_tensor(
                    out=prod[(q, 2)][:, :, hs], in0=xt[(2, c)][:, j0:j0 + n, hs],
                    in1=a_sb[:, 2, hs].unsqueeze(1).to_broadcast([P, n, HALF]), op=ALU.mult)

        def gpsimd_add(q):
            if pre_added(q):
                nc.gpsimd.tensor_tensor(out=prod[(q, 2)][:, :, 0:HALF], in0=prod[(q, 2)][:, :, 0:HALF],
                                        in1=prod[(q, 1)][:, :, 0:HALF], op=ALU.add)

        def vector_share(q):
            n = BLOCKS[q][1]
            c, j0 = where(BLOCKS[q][0])
            for (k, hf) in [(k, hf) for hf in halves(q) for k in (1, 0)]:
                hs = slice(hf * HALF, (hf + 1) * HALF)
                nc.vector.tensor_tensor(
                    out=prod[(q, k)][:, :, hs], in0=xt[(k, c)][:, j0:j0 + n, hs],
                    in1=a_ps[(k, hf)][:].unsqueeze(1).to_broadcast([P, n, HALF]), op=ALU.mult)

        def t_run(q, jj, g):
            n = BLOCKS[q][1]
            if q not in quant:
                quant[q] = (
                    gpool.tile([P, n, 2, P, 4], BF16, tag="grp", name="grp%d" % q, align_bytes=64),
                    gpool.tile([P, n * 2 * P], U32, tag="codes", name="codes%d" % q, align_bytes=64),
                    gpool.tile([P, n * 2 * P], U8, tag="scl", name="scl%d" % q, align_bytes=64),
                )
            acc = psum.tile([P, 4, P], F32, tag="acc", name="acc%d_%d_%d" % (g, q, jj), bufs=2)
            srcs = (2, 0) if (g == 0 and pre_added(q)) else (2, 1, 0)
            for t in range(4):
                col = (4 * g + t) * P
                for k in srcs:
                    nc.tensor.matmul(acc[:, t, :], lhsT=prod[(q, k)][:, jj, col:col + P], rhs=ident_f[:],
                                     is_transpose=True, start=(k == 2), stop=(k == 0))
            nc.scalar.copy(out=quant[q][0][:, jj, g, :, :], in_=acc[:].rearrange("p t b -> p b t"))

        def quantise(q):
            grp, codes, scl = quant[q]
            nc.vector.quantize_mx(out=codes[:].bitcast(FP8X4), scales=scl[:],
                                  in_=grp[:].rearrange("p j g b t -> p (j g b t)"))

        def mx_pair(q, jj, nh):
            codes, scl = quant[q][1], quant[q][2]
            ns = slice(nh * HALF, (nh + 1) * HALF)
            o = psum.tile([P, HALF], F32, tag="o", name="o%d_%d_%d" % (nh, q, jj), bufs=2)
            for g in range(2):
                gs = slice((2 * jj + g) * P, (2 * jj + g + 1) * P)
                nc.tensor.matmul_mx(
                    out=o[:], lhsT=codes[:, gs].bitcast(FP8X4), lhsT_scale=scl[:, gs],
                    rhs=w_codes[:, g, ns].bitcast(FP8X4), rhs_scale=w_scales[:, g, ns],
                    start=(g == 0), stop=(g == 1))
            return o

        def add_bias(q, jj, nh, o):
            ij0, n = BLOCKS[q]
            if (jj, nh) == (0, 0):
                stage[q] = pools["o"].tile([P, n, C], F32, tag="ost", name="ost%d" % q)
            ns = slice(nh * HALF, (nh + 1) * HALF)
            nc.vector.tensor_tensor(out=stage[q][:, jj, ns], in0=o[:], in1=bo_bc[:, ns], op=ALU.add)
            if (jj, nh) == (n - 1, 1):
                nc.sync.dma_start(out=outv[:, ij0:ij0 + n, :], in_=stage[q][:])

        z_tags = (("pa", "pb"), ("pc", "pd"), ("o", "o"))

        with tc.tile_pool(name="head", bufs=1) as head:
            make_identity(nc, ident_b[:])
            make_identity(nc, ident_f[:])

            ba_rows = head.tile([P, NBR * C], BF16, name="ba_rows")
            nc.vector.memset(ba_rows[:], 0.0)
            ones_b = head.tile([P, P], BF16, name="ones_b")
            nc.vector.memset(ones_b[:], 1.0)
            warm = head.tile([P, 1], F32, name="warm")
            nc.vector.memset(warm[:], 0.0)

            gh = head.tile([P, GH], BF16, name="gh")
            nc.sync.dma_start(out=gh[:], in_=gate_hid)
            nc.sync.dma_start(out=ba_rows[0:1, :], in_=ba2.rearrange("(o c) -> o c", o=1))
            wa = head.tile([P, 2, NBR * C], BF16, tag="wa", name="wa", align_bytes=64)
            wav = wa2.rearrange("(kc p) c -> p kc c", p=P)
            for hf in range(2):
                cols = slice(hf * NBR * HALF, (hf + 1) * NBR * HALF)
                nc.sync.dma_start(out=wa[:, :, cols], in_=wav[:, :, cols])
            wo_raw = head.tile([P, 2, 4, C], BF16, name="wo_raw")
            nc.sync.dma_start(out=wo_raw[:], in_=wo.rearrange("(g t p) n -> p g t n", g=2, t=4, p=P))
            for c in range(XBUFS):
                load_chunk(c)
            nc.sync.dma_start(out=bo_bc[:], in_=bo.partition_broadcast(P))

            nc.scalar.activation(out=warm[:], in_=warm[:], func=ACT.Exp)

            ght_ps = psum.tile([P, 2, P], BF16, tag="acc", name="ght_ps", bufs=2)
            for kc in range(2):
                nc.tensor.transpose(ght_ps[:, kc, :], gh[:, kc * P:(kc + 1) * P], ident_b[:])
            ght = head.tile([P, 2, P], BF16, name="ght")
            nc.vector.tensor_copy(out=ght[:], in_=ght_ps[:])

            z = {}
            for hf in range(2):
                cols = slice(hf * NBR * HALF, (hf + 1) * NBR * HALF)
                for k in range(NBR):
                    zt = psum.tile([P, HALF], F32, tag=z_tags[k][hf], name="z%d_%d" % (k, hf),
                                   bufs=(2 if z_tags[k][hf] == "o" else 1))
                    nc.tensor.matmul(
                        zt[:], lhsT=ones_b[:],
                        rhs=ba_rows[:, cols].rearrange("p (c k) -> p c k", k=NBR)[:, :, k],
                        start=True, stop=False)
                    z[(k, hf)] = zt
                for k in range(NBR):
                    for kc in range(2):
                        nc.tensor.matmul(
                            z[(k, hf)][:], lhsT=ght[:, kc, :],
                            rhs=wa[:, kc, cols].rearrange("p (c k) -> p c k", k=NBR)[:, :, k],
                            start=False, stop=(kc == 1))

            wo_grp = [head.tile([P, C, 4], BF16, tag="wa", name="wo_grp0", align_bytes=64),
                      head.tile([P, C, 4], BF16, name="wo_grp1", align_bytes=64)]
            for piece in range(4):
                ns = slice(piece * 256, (piece + 1) * 256)
                nc.gpsimd.tensor_scalar(out=wo_grp[1][:, ns, :],
                                        in0=wo_raw[:, 1, :, ns].rearrange("p t n -> p n t"),
                                        scalar1=1.0, scalar2=0.0, op0=ALU.mult, op1=ALU.add)

            e = {}
            s = {}
            y = {}
            mx = {}
            for hf in range(2):
                mx[hf] = head.tile([P, HALF], F32, name="m_%d" % hf)
                nc.scalar.copy(out=mx[hf][:], in_=z[(0, hf)][:])
            for hf in range(2):
                m = mx[hf]
                nc.vector.tensor_tensor(out=m[:], in0=z[(1, hf)][:], in1=m[:], op=ALU.max)
                nc.vector.tensor_tensor(out=m[:], in0=z[(2, hf)][:], in1=m[:], op=ALU.max)
                e[hf] = head.tile([P, NBR, HALF], F32, name="e_%d" % hf)
                for k in range(NBR):
                    nc.vector.tensor_tensor(out=e[hf][:, k, :], in0=z[(k, hf)][:], in1=m[:], op=ALU.subtract)
                nc.scalar.activation(out=e[hf][:], in_=e[hf][:], func=ACT.Exp)
            for hf in range(2):
                s[hf] = head.tile([P, HALF], F32, name="s_%d" % hf)
                y[hf] = head.tile([P, HALF], F32, name="y_%d" % hf)
                nc.vector.tensor_tensor(out=s[hf][:], in0=e[hf][:, 0, :], in1=e[hf][:, 1, :], op=ALU.add)
                nc.vector.tensor_tensor(out=s[hf][:], in0=s[hf][:], in1=e[hf][:, 2, :], op=ALU.add)
            for hf in range(2):
                nc.scalar.activation(out=y[hf][:], in_=s[hf][:], func=ACT.Abs_reciprocal_sqrt)
                nc.scalar.activation(out=y[hf][:], in_=y[hf][:], func=ACT.Square)
            nc.vector.quantize_mx(out=w_codes[:, 1, :].bitcast(FP8X4), scales=w_scales[:, 1, :],
                                  in_=wo_grp[1][:].rearrange("p n t -> p (n t)"))
            for piece in range(4):
                ns = slice(piece * 256, (piece + 1) * 256)
                nc.scalar.copy(out=wo_grp[0][:, ns, :], in_=wo_raw[:, 0, :, ns].rearrange("p t n -> p n t"))

            for hf in range(2):
                hs = slice(hf * HALF, (hf + 1) * HALF)
                nc.vector.tensor_tensor(out=s[hf][:], in0=s[hf][:], in1=y[hf][:], op=ALU.mult)
                nc.vector.scalar_tensor_tensor(out=y[hf][:], in0=s[hf][:], scalar=2.0, in1=y[hf][:],
                                               op0=ALU.subtract, op1=ALU.mult)
                nc.vector.scalar_tensor_tensor(
                    out=a_sb[:, :, hs], in0=e[hf][:], scalar=-1.0,
                    in1=y[hf][:].unsqueeze(1).to_broadcast([P, NBR, HALF]), op0=ALU.mult, op1=ALU.mult)
                for k in (1, 0):
                    ap = psum.tile([P, HALF], F32, tag=z_tags[k][hf], name="aps%d_%d" % (k, hf))
                    nc.tensor.matmul(ap[:], lhsT=ident_f[:], rhs=a_sb[:, k, hs], start=True, stop=True)
                    a_ps[(k, hf)] = ap

            for q in range(2):
                new_products(q)
                gpsimd_share(q)
            for q in range(2):
                vector_share(q)
                gpsimd_add(q)
                load_after(q)
            nc.vector.quantize_mx(out=w_codes[:, 0, :].bitcast(FP8X4), scales=w_scales[:, 0, :],
                                  in_=wo_grp[0][:].rearrange("p n t -> p (n t)"))

        pools["o"] = ctx.enter_context(tc.tile_pool(name="opool", bufs=3))

        for q in range(NB + 1):
            if q < NB:
                for g in halves(q):
                    for jj in range(BLOCKS[q][1]):
                        t_run(q, jj, g)
            pairs = [(jj, nh) for jj in range(BLOCKS[q - 1][1]) for nh in range(2)] if q >= 1 else []
            for (jj, nh) in pairs[:2]:
                add_bias(q - 1, jj, nh, mx_pair(q - 1, jj, nh))
            if q < NB:
                quantise(q)
            if q + 2 < NB:
                new_products(q + 2)
                touch(q + 2)
                gpsimd_share(q + 2)
            for (jj, nh) in pairs[2:]:
                add_bias(q - 1, jj, nh, mx_pair(q - 1, jj, nh))
            if q + 2 < NB:
                vector_share(q + 2)
                gpsimd_add(q + 2)
                load_after(q + 2)
